import numpy as np
import ml_dtypes


def mxq(x, axis, fmt="e4m3"):
    dtype, down = {"e4m3": (ml_dtypes.float8_e4m3fn, 7), "e5m2": (ml_dtypes.float8_e5m2, 14)}[fmt]
    v = np.moveaxis(np.asarray(x, np.float32).astype(ml_dtypes.bfloat16).astype(np.float64), axis, -1)
    blocks = v.reshape(v.shape[:-1] + (-1, 32))
    amax = np.abs(blocks).max(-1, keepdims=True)
    byte = np.maximum(np.where(amax > 0, np.frexp(amax)[1] - 1 + 127, 0) - down, 1)
    scale = np.exp2(byte - 127.0)
    codes = (blocks / scale).astype(np.float32).astype(dtype).astype(np.float64)
    return np.moveaxis((codes * scale).reshape(v.shape), -1, axis)


WIDE = False


def mx_kscale(k):
    if not WIDE:
        return np.ones(k)
    levels = np.array([10, -10, 5, -5, 0])
    if k % 512:
        return np.exp2(np.random.permutation(np.resize(levels, k // 32))).repeat(32)
    a = np.empty((k // 512, 16))
    for p in range(k // 512):
        a[p, :8] = np.random.permutation(np.resize(levels, 8))
        for g in range(8):
            far = levels[np.abs(levels - a[p, g]) >= 10]
            a[p, g + 8] = far[np.random.randint(len(far))]
    return np.exp2(a.ravel()).repeat(32)


BF16 = ml_dtypes.bfloat16


def bf(x):
    return np.asarray(x, np.float32).astype(BF16)


def f64(x):
    return np.asarray(x).astype(np.float64)


E2M1 = np.array([0.0, 0.5, 1.0, 1.5, 2.0, 3.0, 4.0, 6.0, -0.0, -0.5, -1.0, -1.5, -2.0, -3.0, -4.0, -6.0])


def pack_weight(w, fmt):
    k, n = w.shape
    w = f64(bf(w)).reshape(k // 32, 32, n)
    amax = np.abs(w).max(1)
    if fmt == "e4m3":
        byte = np.frexp(amax)[1] - 1 + 127 - 7
    else:
        mant, ex = np.frexp(amax / 6.0)
        byte = np.where(mant > 0.5, ex, ex - 1) + 127
    byte = np.clip(np.where(amax > 0, byte, 1), 1, 254)
    scaled = (w * np.exp2(127.0 - byte)[:, None, :]).reshape(k, n).astype(np.float32)
    by_word = np.ascontiguousarray(scaled.reshape(k // 512, 128, 4, n).transpose(0, 1, 3, 2))
    if fmt == "e4m3":
        words = by_word.astype(ml_dtypes.float8_e4m3fn).view(np.uint8)
    else:
        c = by_word.astype(ml_dtypes.float4_e2m1fn).view(np.uint8) & 0xF
        words = c[..., 0::2] | (c[..., 1::2] << 4)
    return np.ascontiguousarray(words), np.ascontiguousarray(byte.astype(np.uint8).reshape(k // 512, 16, n))


def unpack_weight(words, scales, fmt):
    g, p, n, _ = words.shape
    if fmt == "e4m3":
        vals = np.ascontiguousarray(words).view(ml_dtypes.float8_e4m3fn).astype(np.float64)
    else:
        nib = np.empty((g, p, n, 4), np.uint8)
        nib[..., 0::2] = words & 0xF
        nib[..., 1::2] = words >> 4
        vals = E2M1[nib]
    vals = vals * np.repeat(np.exp2(scales.astype(np.float64) - 127.0), 8, axis=1)[..., None]
    return vals.transpose(0, 1, 3, 2).reshape(g * 512, n)
def pack4(w):
    words, scales = pack_weight(w, "e2m1")
    return words.reshape(words.shape[0], 128, -1), scales


def unpack4(words, scales):
    return unpack_weight(words.reshape(words.shape[0], 128, -1, 2), scales, "e2m1")


B, S, D, H, E, LAYERS, PLEN = 4, 1024, 1024, 8, 1024, 32, 4
LQ = LAYERS * PLEN


def draw0():
    s, t = mx_kscale(D), mx_kscale(D)
    common = np.random.standard_normal((1, 1, D)) * 0.2
    pos_o = bf((common + np.random.standard_normal((B, LQ, D)) * 0.2) * s)
    neg_o = bf((common + np.random.standard_normal((B, LQ, D)) * 0.07) * s)
    Wo_words, Wo_scales = pack4(np.random.standard_normal((D, D)) * 2.0 / np.sqrt(D) / s[:, None] * t)
    bo = bf(np.random.standard_normal(D) * 0.2 * t)
    Wp_words, Wp_scales = pack4(np.random.standard_normal((D, E)) * 1.5 / np.sqrt(D) / t[:, None])
    bp = bf(np.random.standard_normal(E) * 0.2)
    return {"pos_o": pos_o,
            "neg_o": neg_o,
            "Wo_words": Wo_words,
            "Wo_scales": Wo_scales,
            "bo": bo,
            "Wp_words": Wp_words,
            "Wp_scales": Wp_scales,
            "bp": bp}


def core(pos_o, neg_o, Wo_words, Wo_scales, bo, Wp_words, Wp_scales, bp):
    woq = unpack4(Wo_words, Wo_scales)
    wpq = unpack4(Wp_words, Wp_scales)
    pos_h = (mxq(f64(pos_o), 2, "e4m3") @ woq) + f64(bo)
    neg_h = (mxq(f64(neg_o), 2, "e4m3") @ woq) + f64(bo)
    pos_p = (mxq(pos_h, 2, "e4m3") @ wpq) + f64(bp)
    neg_p = (mxq(neg_h, 2, "e4m3") @ wpq) + f64(bp)
    xy = np.sum(pos_p * neg_p, axis=-1, keepdims=True)
    xx = np.sum(pos_p * pos_p, axis=-1, keepdims=True)
    neg_p = neg_p - (xy / (xx + 1e-8)) * pos_p
    return pos_p.reshape(B, LAYERS, PLEN, E), neg_p.reshape(B, LAYERS, PLEN, E)


def e4m3fn_bytes(y):
    return np.clip(np.asarray(y, np.float64), -448.0, 448.0).astype(np.float32).astype(ml_dtypes.float8_e4m3fn).view(np.uint8)


def e4m3fn_values(b):
    return np.asarray(b, np.uint8).view(ml_dtypes.float8_e4m3fn).astype(np.float64)


def setup_inputs():
    d = draw0()
    x0 = np.asarray(d['pos_o']).astype(np.float64)
    s = (np.max(np.abs(x0), axis=(0, 1), keepdims=True) / 448.0).astype(np.float32)
    out = {}
    for k, v in d.items():
        if k == 'pos_o':
            out['pos_o_bytes'] = e4m3fn_bytes(x0 / s.astype(np.float64))
            out['pos_o_scale'] = s
        else:
            out[k] = v
    return out


def reference(pos_o_bytes, pos_o_scale, neg_o, Wo_words, Wo_scales, bo, Wp_words, Wp_scales, bp):
    return core(e4m3fn_values(pos_o_bytes) * pos_o_scale.astype(np.float64), neg_o, Wo_words, Wo_scales, bo, Wp_words, Wp_scales, bp)

@@ -1,0 +1,297 @@
+from contextlib import ExitStack
+
+import concourse.mybir as mybir
+from concourse.masks import make_identity
+
+F32 = mybir.dt.float32
+BF16 = mybir.dt.bfloat16
+I32 = mybir.dt.int32
+U32 = mybir.dt.uint32
+U8 = mybir.dt.uint8
+F8 = mybir.dt.float8_e4m3fn
+FP8X4 = mybir.dt.float8_e4m3fn_x4
+FP4X4 = mybir.dt.float4_e2m1fn_x4
+ADD = mybir.AluOpType.add
+SUB = mybir.AluOpType.subtract
+MULT = mybir.AluOpType.mult
+SQUARE = mybir.ActivationFunctionType.Square
+IDENTITY = mybir.ActivationFunctionType.Identity
+
+P = 128
+R = 4
+K = 1024
+G = 2
+EPS = 1e-8
+FLOPS = 4 * 2 * 512 * 1024 * 1024
+NEG, POS = 0, 1
+HID_GPSIMD = ()
+HID_SCALAR = tuple((NEG, r, 1) for r in range(R))
+POS_VECTOR = (3,)
+
+
+def tile_qkvorthoposnegpromptg_pb_w4_kernel(
+    tc, pos_o_bytes, pos_o_scale, neg_o, Wo_words, Wo_scales, bo, Wp_words, Wp_scales, bp, out_0, out_1
+):
+    nc = tc.nc
+    with ExitStack() as ctx:
+        keep = ctx.enter_context(tc.tile_pool(name="keep", bufs=1))
+        work = ctx.enter_context(tc.tile_pool(name="work", bufs=4))
+        psum = ctx.enter_context(tc.psum_pool(name="psum", bufs=8))
+        ctx.enter_context(tc.manual_schedule())
+
+        wos = keep.tile([P, G * K], U8, align_bytes=64)
+        wps = keep.tile([P, G * K], U8, align_bytes=64)
+        dummy = keep.tile([P, 8], F32)
+        ident = keep.tile([P, P], F32)
+        nc.vector.memset(wos[:].bitcast(I32), 0)
+        nc.vector.memset(dummy[:], 1.0)
+        nc.vector.memset(wps[:].bitcast(I32), 0)
+        make_identity(nc, ident[:])
+        dummy2 = keep.tile([P, 8], F32)
+
+        xn = [keep.tile([P, K], BF16, name="xn%d" % r, align_bytes=64) for r in range(R)]
+        xb = [keep.tile([P, K], U8, name="xb%d" % r, align_bytes=64) for r in range(R)]
+        wow = keep.tile([P, 2, G, 1024], U8, align_bytes=64)
+        wpw = keep.tile([P, G, 2048], U8, align_bytes=64)
+        sc = keep.tile([P, G, 4], F32)
+        bpt = keep.tile([P, K], BF16)
+        bot = keep.tile([P, 2, 4], BF16)
+        nbot = keep.tile([P, 2, 4], F32)
+
+        nc.scalar.dma_start(out=xn[0][:], in_=neg_o[0])
+        nc.scalar.dma_start(out=bot[:], in_=bo.rearrange("(g p t) -> p g t", p=P, t=4))
+        nc.scalar.dma_start(out=sc[:], in_=pos_o_scale.rearrange("a b (g p t) -> p (a b g) t", p=P, t=4))
+        nc.scalar.activation(dummy2[:], dummy[:], SQUARE)
+
+        def load_scales(tile, dram):
+            for q in range(4):
+                nc.sync.dma_start(
+                    out=tile[32 * q : 32 * q + 4, :].bitcast(I32).rearrange("q (g n) -> q g n", g=G),
+                    in_=dram[:, 4 * q : 4 * q + 4, :].rearrange("g q n -> q g n").bitcast(I32),
+                )
+
+        load_scales(wos, Wo_scales)
+        for c in range(2):
+            nc.sync.dma_start(out=wow[:, c], in_=Wo_words[:, :, 1024 * c : 1024 * (c + 1)].rearrange("g p b -> p g b"))
+            if c == 0:
+                nc.sync.dma_start(out=xn[1][:], in_=neg_o[1])
+                nc.sync.dma_start(out=xb[0][:], in_=pos_o_bytes[0])
+        nc.sync.dma_start(out=xb[1][:], in_=pos_o_bytes[1])
+        for r in range(2, R):
+            nc.sync.dma_start(out=xn[r][:], in_=neg_o[r])
+            nc.sync.dma_start(out=xb[r][:], in_=pos_o_bytes[r])
+        load_scales(wps, Wp_scales)
+        nc.sync.dma_start(out=wpw[:], in_=Wp_words.rearrange("g p b -> p g b"))
+        nc.sync.dma_start(out=bpt[:], in_=bp.partition_broadcast(P))
+        nc.gpsimd.tensor_scalar(
+            out=nbot[:].rearrange("p g t -> p (g t)"), in0=bot[:].rearrange("p g t -> p (g t)"), scalar1=-1.0,
+            scalar2=0.0, op0=MULT, op1=ADD,
+        )
+
+        wop = keep.tile([P, 2, G, 4, 256], U8, align_bytes=64)
+        wosp = keep.tile([P, 2, G, 4, P], U8, align_bytes=64)
+        xp, xw, xq, xs, hb, hq, hs, pt, xxt = {}, {}, {}, {}, {}, {}, {}, {}, {}
+        bank, st, junk, ot = {}, {}, {}, {}
+
+        def perm_scales(c):
+            nc.vector.tensor_copy(
+                out=wosp[:, c], in_=wos[:].rearrange("p (g c m t) -> p c g t m", g=G, c=2, t=4)[:, c]
+            )
+
+        def perm_words(c):
+            nc.vector.tensor_copy(
+                out=wop[:, c].rearrange("p g t (m b) -> p g t m b", b=2),
+                in_=wow[:, c].rearrange("p g (m t b) -> p g t m b", t=4, b=2),
+            )
+
+        def widen(r):
+            xp[r] = work.tile([P, K], BF16, name="xp", align_bytes=64)
+            nc.scalar.copy(out=xp[r][:], in_=xb[r][:].bitcast(F8))
+
+        def turn(s, r):
+            words = (xp[r] if s else xn[r])[:].bitcast(F32)
+            b = bank["x", s, r] = psum.tile([P, 512], F32, name="bank")
+            for g in range(G):
+                for u in range(2):
+                    j = 2 * g + u
+                    nc.tensor.transpose(b[:, P * j : P * (j + 1)], words[:, 256 * g + u : 256 * (g + 1) : 2], ident[:])
+
+        def take(s, r):
+            b = bank["x", s, r]
+            xw[s, r] = work.tile([P, G, P, 4], BF16, name="xw", align_bytes=64)
+            if s == NEG:
+                nc.scalar.copy(
+                    out=xw[s, r][:].rearrange("p g r k -> p (g r k)").bitcast(F32).rearrange("p (g r u) -> p g r u", g=G, u=2),
+                    in_=b[:].rearrange("p (g u r) -> p g r u", g=G, u=2),
+                )
+            else:
+                for g in range(G):
+                    nc.vector.tensor_tensor(
+                        out=xw[s, r][:, g].rearrange("p r (u e) -> p r u e", e=2),
+                        in0=b[:, 256 * g : 256 * (g + 1)].bitcast(BF16).rearrange("p (u r e) -> p r u e", u=2, e=2),
+                        in1=sc[:, g : g + 1, :].rearrange("p g (u e) -> p g u e", e=2).to_broadcast([P, P, 2, 2]),
+                        op=MULT,
+                    )
+
+        def quant(s, r, src, codes, planes, bufs):
+            codes[s, r] = work.tile([P, 256], U32, name="q", bufs=16, align_bytes=64)
+            planes[s, r] = work.tile([P, 256], U8, name="s", bufs=16, align_bytes=64)
+            nc.vector.quantize_mx(
+                out=codes[s, r][:].bitcast(FP8X4), scales=planes[s, r][:], in_=src.rearrange("p g r k -> p (g r k)")
+            )
+
+        def quant_x(s, r):
+            quant(s, r, xw[s, r][:], xq, xs, 8)
+
+        def quant_h(s, r):
+            quant(s, r, hb[s, r][:], hq, hs, 8)
+
+        def hidden(s, r, c):
+            b = bank["h", s, r, c] = psum.tile([P, 512], F32, name="bank")
+            for t in range(4):
+                for g in range(G):
+                    cols = slice(P * g, P * (g + 1))
+                    nc.tensor.matmul_mx(
+                        out=b[:, P * t : P * (t + 1)],
+                        lhsT=wop[:, c, g, t, :].bitcast(FP4X4),
+                        lhsT_scale=wosp[:, c, g, t, :],
+                        rhs=xq[s, r][:, cols].bitcast(FP8X4),
+                        rhs_scale=xs[s, r][:, cols],
+                        start=(g == 0),
+                        stop=(g == G - 1),
+                    )
+
+        def add_bias(s, r, c):
+            if (s, r) not in hb:
+                hb[s, r] = work.tile([P, 2, P, 4], BF16, name="hb", align_bytes=64)
+            dst = hb[s, r][:, c]
+            src = bank["h", s, r, c][:].rearrange("p (t n) -> p n t", t=4)
+            if (s, r, c) in HID_SCALAR:
+                for t in range(4):
+                    nc.scalar.activation(
+                        dst[:, :, t], src[:, :, t], IDENTITY, bias=nbot[:, c, t : t + 1], scale=1.0 if s else -1.0
+                    )
+                return
+            eng = nc.vector
+            if (s, r, c) in HID_GPSIMD:
+                raw = work.tile([P, P, 4], F32, name="raw")
+                nc.scalar.copy(out=raw[:], in_=src)
+                src = raw[:]
+                eng = nc.gpsimd
+            if s:
+                eng.tensor_tensor(out=dst, in0=src, in1=bot[:, c : c + 1, :].to_broadcast([P, P, 4]), op=ADD)
+            else:
+                eng.tensor_tensor(out=dst, in0=nbot[:, c : c + 1, :].to_broadcast([P, P, 4]), in1=src, op=SUB)
+
+        def project(key, r, e, streams):
+            b = bank[key, r, e] = psum.tile([P, 512], F32, name="bank")
+            passes = [(s, g) for s in streams for g in range(G)]
+            for s, g in passes:
+                cols = slice(P * g, P * (g + 1))
+                nc.tensor.matmul_mx(
+                    out=b[:],
+                    lhsT=hq[s, r][:, cols].bitcast(FP8X4),
+                    lhsT_scale=hs[s, r][:, cols],
+                    rhs=wpw[:, g, 1024 * e : 1024 * (e + 1)].bitcast(FP4X4),
+                    rhs_scale=wps[:, K * g + 512 * e : K * g + 512 * (e + 1)],
+                    start=(s, g) == passes[0],
+                    stop=(s, g) == passes[-1],
+                )
+
+        def pos_bank(r, e):
+            project("p", r, e, (POS,))
+
+        def diff_bank(r, e):
+            project("d", r, e, (POS, NEG))
+
+        def half(e):
+            return slice(512 * e, 512 * (e + 1))
+
+        def pos_out(r, e):
+            if e == 0:
+                pt[r] = work.tile([P, K], F32, name="pt")
+                xxt[r] = work.tile([P, 2], F32, name="xx")
+            if r in POS_VECTOR:
+                nc.vector.tensor_tensor(out=pt[r][:, half(e)], in0=bank["p", r, e][:], in1=bpt[:, half(e)], op=ADD)
+            else:
+                raw = work.tile([P, P, 4], F32, name="raw")
+                flat = raw[:].rearrange("p n t -> p (n t)")
+                nc.scalar.copy(out=flat, in_=bank["p", r, e][:])
+                nc.gpsimd.tensor_tensor(out=pt[r][:, half(e)], in0=flat, in1=bpt[:, half(e)], op=ADD)
+            nc.sync.dma_start(out=out_0[r].rearrange("l p e -> (l p) e")[:, half(e)], in_=pt[r][:, half(e)])
+
+        def square(r, e):
+            sq = work.tile([P, 512], F32, name="sq", bufs=2)
+            nc.scalar.activation(sq[:], pt[r][:, half(e)], SQUARE, accum_out=xxt[r][:, e : e + 1])
+
+        def dot(r, e):
+            if e == 0:
+                st[r] = work.tile([P, 8], F32, name="st")
+            jk = work.tile([P, 512], F32, name="junk", bufs=2)
+            nc.vector.scalar_tensor_tensor(
+                out=jk[:], in0=bank["d", r, e][:], scalar=1.0, in1=pt[r][:, half(e)], op0=MULT, op1=MULT,
+                accum_out=st[r][:, e : e + 1],
+            )
+
+        def coeff(r):
+            s = st[r]
+            nc.vector.scalar_tensor_tensor(
+                out=s[:, 2:3], in0=xxt[r][:, 0:1], scalar=EPS, in1=xxt[r][:, 1:2], op0=ADD, op1=ADD
+            )
+            nc.vector.tensor_scalar(out=s[:, 4:5], in0=s[:, 0:1], scalar1=EPS, scalar2=None, op0=ADD)
+            nc.vector.reciprocal(s[:, 3:4], s[:, 2:3])
+            nc.vector.tensor_scalar(
+                out=s[:, 5:6], in0=s[:, 1:2], scalar1=s[:, 4:5], scalar2=s[:, 3:4], op0=ADD, op1=MULT
+            )
+
+        def neg_out(r, e):
+            if e == 0:
+                ot[r] = work.tile([P, K], F32, name="ot")
+            nc.vector.scalar_tensor_tensor(
+                out=ot[r][:, half(e)], in0=pt[r][:, half(e)], scalar=st[r][:, 5:6], in1=bank["d", r, e][:],
+                op0=MULT, op1=SUB,
+            )
+            nc.sync.dma_start(out=out_1[r].rearrange("l p e -> (l p) e")[:, half(e)], in_=ot[r][:, half(e)])
+
+        turn(NEG, 0)
+        widen(0)
+        take(NEG, 0)
+        for c in range(2):
+            perm_scales(c)
+            perm_words(c)
+        for r in range(1, R):
+            widen(r)
+        for r in range(R):
+            if r + 1 < R:
+                turn(NEG, r + 1)
+            turn(POS, r)
+            if r + 1 < R:
+                take(NEG, r + 1)
+            take(POS, r)
+            quant_x(NEG, r)
+            quant_x(POS, r)
+        for i in range(R + 2):
+            j = i - 2
+            if i < R:
+                for c in (1, 0):
+                    hidden(NEG, i, c)
+                    hidden(POS, i, c)
+                for c in (1, 0):
+                    add_bias(NEG, i, c)
+                    add_bias(POS, i, c)
+                quant_h(NEG, i)
+            if j >= 0:
+                for e in range(2):
+                    pos_bank(j, e)
+                    pos_out(j, e)
+                for e in range(2):
+                    diff_bank(j, e)
+                    square(j, e)
+                for e in range(2):
+                    dot(j, e)
+                coeff(j)
+            if i < R:
+                quant_h(POS, i)
+            if j >= 0:
+                for e in range(2):
+                    neg_out(j, e)

@@ -50,7 +50,7 @@ def tile_qkvorthoposnegpromptg_pb_w4_kernel(
         dummy2 = keep.tile([P, 8], F32)
 
         xn = [keep.tile([P, K], BF16, name="xn%d" % r, align_bytes=64) for r in range(R)]
-        xb = [keep.tile([P, K], U8, name="xb%d" % r, align_bytes=64) for r in range(R)]
+        xb = keep.tile([P, R, K], U8, align_bytes=64)
         wow = keep.tile([P, 2, G, 1024], U8, align_bytes=64)
         wpw = keep.tile([P, G, 2048], U8, align_bytes=64)
         sc = keep.tile([P, G, 4], F32)
@@ -59,8 +59,6 @@ def tile_qkvorthoposnegpromptg_pb_w4_kernel(
         nbot = keep.tile([P, 2, 4], F32)
 
         nc.scalar.dma_start(out=xn[0][:], in_=neg_o[0])
-        nc.scalar.dma_start(out=bot[:], in_=bo.rearrange("(g p t) -> p g t", p=P, t=4))
-        nc.scalar.dma_start(out=sc[:], in_=pos_o_scale.rearrange("a b (g p t) -> p (a b g) t", p=P, t=4))
         nc.scalar.activation(dummy2[:], dummy[:], SQUARE)
 
         def load_scales(tile, dram):
@@ -70,16 +68,22 @@ def tile_qkvorthoposnegpromptg_pb_w4_kernel(
                     in_=dram[:, 4 * q : 4 * q + 4, :].rearrange("g q n -> q g n").bitcast(I32),
                 )
 
-        load_scales(wos, Wo_scales)
-        for c in range(2):
+        def load_wo(c):
             nc.sync.dma_start(out=wow[:, c], in_=Wo_words[:, :, 1024 * c : 1024 * (c + 1)].rearrange("g p b -> p g b"))
-            if c == 0:
-                nc.sync.dma_start(out=xn[1][:], in_=neg_o[1])
-                nc.sync.dma_start(out=xb[0][:], in_=pos_o_bytes[0])
-        nc.sync.dma_start(out=xb[1][:], in_=pos_o_bytes[1])
+
+        def load_pos(r):
+            nc.sync.dma_start(out=xb[:, r : r + 2], in_=pos_o_bytes[r : r + 2].rearrange("r p k -> p r k"))
+
+        load_wo(1)
+        load_wo(0)
+        load_pos(0)
+        load_scales(wos, Wo_scales)
+        nc.sync.dma_start(out=xn[1][:], in_=neg_o[1])
+        nc.sync.dma_start(out=sc[:], in_=pos_o_scale.rearrange("a b (g p t) -> p (a b g) t", p=P, t=4))
+        load_pos(2)
+        nc.sync.dma_start(out=bot[:], in_=bo.rearrange("(g p t) -> p g t", p=P, t=4))
         for r in range(2, R):
             nc.sync.dma_start(out=xn[r][:], in_=neg_o[r])
-            nc.sync.dma_start(out=xb[r][:], in_=pos_o_bytes[r])
         load_scales(wps, Wp_scales)
         nc.sync.dma_start(out=wpw[:], in_=Wp_words.rearrange("g p b -> p g b"))
         nc.sync.dma_start(out=bpt[:], in_=bp.partition_broadcast(P))
@@ -106,7 +110,7 @@ def tile_qkvorthoposnegpromptg_pb_w4_kernel(
 
         def widen(r):
             xp[r] = work.tile([P, K], BF16, name="xp", align_bytes=64)
-            nc.scalar.copy(out=xp[r][:], in_=xb[r][:].bitcast(F8))
+            nc.scalar.copy(out=xp[r][:], in_=xb[:, r].bitcast(F8))
 
         def turn(s, r):
             words = (xp[r] if s else xn[r])[:].bitcast(F32)
@@ -233,13 +237,19 @@ def tile_qkvorthoposnegpromptg_pb_w4_kernel(
                 accum_out=st[r][:, e : e + 1],
             )
 
+        def den(r):
+            nc.vector.scalar_tensor_tensor(
+                out=st[r][:, 2:3], in0=xxt[r][:, 0:1], scalar=EPS, in1=xxt[r][:, 1:2], op0=ADD, op1=ADD
+            )
+
+        def first_dot(r):
+            nc.vector.tensor_scalar(out=st[r][:, 4:5], in0=st[r][:, 0:1], scalar1=EPS, scalar2=None, op0=ADD)
+
+        def inverse(r):
+            nc.vector.reciprocal(st[r][:, 3:4], st[r][:, 2:3])
+
         def coeff(r):
             s = st[r]
-            nc.vector.scalar_tensor_tensor(
-                out=s[:, 2:3], in0=xxt[r][:, 0:1], scalar=EPS, in1=xxt[r][:, 1:2], op0=ADD, op1=ADD
-            )
-            nc.vector.tensor_scalar(out=s[:, 4:5], in0=s[:, 0:1], scalar1=EPS, scalar2=None, op0=ADD)
-            nc.vector.reciprocal(s[:, 3:4], s[:, 2:3])
             nc.vector.tensor_scalar(
                 out=s[:, 5:6], in0=s[:, 1:2], scalar1=s[:, 4:5], scalar2=s[:, 3:4], op0=ADD, op1=MULT
             )
@@ -254,44 +264,61 @@ def tile_qkvorthoposnegpromptg_pb_w4_kernel(
             nc.sync.dma_start(out=out_1[r].rearrange("l p e -> (l p) e")[:, half(e)], in_=ot[r][:, half(e)])
 
         turn(NEG, 0)
-        widen(0)
         take(NEG, 0)
-        for c in range(2):
-            perm_scales(c)
+        for c in (1, 0):
             perm_words(c)
-        for r in range(1, R):
+        for c in (1, 0):
+            perm_scales(c)
+        for r in range(R):
             widen(r)
+        quant_x(NEG, 0)
         for r in range(R):
             if r + 1 < R:
                 turn(NEG, r + 1)
-            turn(POS, r)
-            if r + 1 < R:
                 take(NEG, r + 1)
+            turn(POS, r)
+        for r in range(R):
             take(POS, r)
-            quant_x(NEG, r)
+            if r + 1 < R:
+                quant_x(NEG, r + 1)
             quant_x(POS, r)
-        for i in range(R + 2):
-            j = i - 2
-            if i < R:
-                for c in (1, 0):
-                    hidden(NEG, i, c)
-                    hidden(POS, i, c)
-                for c in (1, 0):
-                    add_bias(NEG, i, c)
-                    add_bias(POS, i, c)
-                quant_h(NEG, i)
-            if j >= 0:
+        for i in range(R):
+            for c in (1, 0):
+                hidden(NEG, i, c)
+                hidden(POS, i, c)
+            add_bias(NEG, i, 1)
+            add_bias(POS, i, 1)
+            if i > 0:
+                quant_h(POS, i - 1)
+            add_bias(NEG, i, 0)
+            if i > 0:
+                quant_h(NEG, i - 1)
+            add_bias(POS, i, 0)
+            if i == R - 2:
                 for e in range(2):
-                    pos_bank(j, e)
-                    pos_out(j, e)
-                for e in range(2):
+                    pos_bank(0, e)
+                    pos_out(0, e)
+                square(0, 0)
+        for j in range(R + 1):
+            for e in range(2):
+                if j < R:
                     diff_bank(j, e)
-                    square(j, e)
-                for e in range(2):
                     dot(j, e)
+                if (j, e) == (0, 0):
+                    quant_h(POS, R - 1)
+                    quant_h(NEG, R - 1)
+                if j + 1 < R:
+                    pos_bank(j + 1, e)
+                    pos_out(j + 1, e)
+                if j < R and e == 0:
+                    square(j, 1)
+                    den(j)
+                if j + 1 < R and e == 1:
+                    square(j + 1, 0)
+                if j < R and e == 1:
+                    first_dot(j)
+                    inverse(j)
+                if j > 0:
+                    neg_out(j - 1, e)
+            if j < R:
                 coeff(j)
-            if i < R:
-                quant_h(POS, i)
-            if j >= 0:
-                for e in range(2):
-                    neg_out(j, e)

from contextlib import ExitStack

import concourse.mybir as mybir
from concourse.masks import make_identity

F32 = mybir.dt.float32
BF16 = mybir.dt.bfloat16
I32 = mybir.dt.int32
U32 = mybir.dt.uint32
U8 = mybir.dt.uint8
F8 = mybir.dt.float8_e4m3fn
FP8X4 = mybir.dt.float8_e4m3fn_x4
FP4X4 = mybir.dt.float4_e2m1fn_x4
ADD = mybir.AluOpType.add
SUB = mybir.AluOpType.subtract
MULT = mybir.AluOpType.mult
SQUARE = mybir.ActivationFunctionType.Square
IDENTITY = mybir.ActivationFunctionType.Identity

P = 128
R = 4
K = 1024
G = 2
EPS = 1e-8
FLOPS = 4 * 2 * 512 * 1024 * 1024
NEG, POS = 0, 1
HID_GPSIMD = ()
HID_SCALAR = tuple((NEG, r, 1) for r in range(R))
POS_VECTOR = (3,)


def tile_qkvorthoposnegpromptg_pb_w4_kernel(
    tc, pos_o_bytes, pos_o_scale, neg_o, Wo_words, Wo_scales, bo, Wp_words, Wp_scales, bp, out_0, out_1
):
    nc = tc.nc
    with ExitStack() as ctx:
        keep = ctx.enter_context(tc.tile_pool(name="keep", bufs=1))
        work = ctx.enter_context(tc.tile_pool(name="work", bufs=4))
        psum = ctx.enter_context(tc.psum_pool(name="psum", bufs=8))
        ctx.enter_context(tc.manual_schedule())

        wos = keep.tile([P, G * K], U8, align_bytes=64)
        wps = keep.tile([P, G * K], U8, align_bytes=64)
        dummy = keep.tile([P, 8], F32)
        ident = keep.tile([P, P], F32)
        nc.vector.memset(wos[:].bitcast(I32), 0)
        nc.vector.memset(dummy[:], 1.0)
        nc.vector.memset(wps[:].bitcast(I32), 0)
        make_identity(nc, ident[:])
        dummy2 = keep.tile([P, 8], F32)

        xn = [keep.tile([P, K], BF16, name="xn%d" % r, align_bytes=64) for r in range(R)]
        xb = keep.tile([P, R, K], U8, align_bytes=64)
        wow = keep.tile([P, 2, G, 1024], U8, align_bytes=64)
        wpw = keep.tile([P, G, 2048], U8, align_bytes=64)
        sc = keep.tile([P, G, 4], F32)
        bpt = keep.tile([P, K], BF16)
        bot = keep.tile([P, 2, 4], BF16)
        nbot = keep.tile([P, 2, 4], F32)

        nc.scalar.dma_start(out=xn[0][:], in_=neg_o[0])
        nc.scalar.activation(dummy2[:], dummy[:], SQUARE)

        def load_scales(tile, dram):
            for q in range(4):
                nc.sync.dma_start(
                    out=tile[32 * q : 32 * q + 4, :].bitcast(I32).rearrange("q (g n) -> q g n", g=G),
                    in_=dram[:, 4 * q : 4 * q + 4, :].rearrange("g q n -> q g n").bitcast(I32),
                )

        def load_wo(c):
            nc.sync.dma_start(out=wow[:, c], in_=Wo_words[:, :, 1024 * c : 1024 * (c + 1)].rearrange("g p b -> p g b"))

        def load_pos(r):
            nc.sync.dma_start(out=xb[:, r : r + 2], in_=pos_o_bytes[r : r + 2].rearrange("r p k -> p r k"))

        load_wo(1)
        load_wo(0)
        load_pos(0)
        load_scales(wos, Wo_scales)
        nc.sync.dma_start(out=xn[1][:], in_=neg_o[1])
        nc.sync.dma_start(out=sc[:], in_=pos_o_scale.rearrange("a b (g p t) -> p (a b g) t", p=P, t=4))
        load_pos(2)
        nc.sync.dma_start(out=bot[:], in_=bo.rearrange("(g p t) -> p g t", p=P, t=4))
        for r in range(2, R):
            nc.sync.dma_start(out=xn[r][:], in_=neg_o[r])
        load_scales(wps, Wp_scales)
        nc.sync.dma_start(out=wpw[:], in_=Wp_words.rearrange("g p b -> p g b"))
        nc.sync.dma_start(out=bpt[:], in_=bp.partition_broadcast(P))
        nc.gpsimd.tensor_scalar(
            out=nbot[:].rearrange("p g t -> p (g t)"), in0=bot[:].rearrange("p g t -> p (g t)"), scalar1=-1.0,
            scalar2=0.0, op0=MULT, op1=ADD,
        )

        wop = keep.tile([P, 2, G, 4, 256], U8, align_bytes=64)
        wosp = keep.tile([P, 2, G, 4, P], U8, align_bytes=64)
        xp, xw, xq, xs, hb, hq, hs, pt, xxt = {}, {}, {}, {}, {}, {}, {}, {}, {}
        bank, st, junk, ot = {}, {}, {}, {}

        def perm_scales(c):
            nc.vector.tensor_copy(
                out=wosp[:, c], in_=wos[:].rearrange("p (g c m t) -> p c g t m", g=G, c=2, t=4)[:, c]
            )

        def perm_words(c):
            nc.vector.tensor_copy(
                out=wop[:, c].rearrange("p g t (m b) -> p g t m b", b=2),
                in_=wow[:, c].rearrange("p g (m t b) -> p g t m b", t=4, b=2),
            )

        def widen(r):
            xp[r] = work.tile([P, K], BF16, name="xp", align_bytes=64)
            nc.scalar.copy(out=xp[r][:], in_=xb[:, r].bitcast(F8))

        def turn(s, r):
            words = (xp[r] if s else xn[r])[:].bitcast(F32)
            b = bank["x", s, r] = psum.tile([P, 512], F32, name="bank")
            for g in range(G):
                for u in range(2):
                    j = 2 * g + u
                    nc.tensor.transpose(b[:, P * j : P * (j + 1)], words[:, 256 * g + u : 256 * (g + 1) : 2], ident[:])

        def take(s, r):
            b = bank["x", s, r]
            xw[s, r] = work.tile([P, G, P, 4], BF16, name="xw", align_bytes=64)
            if s == NEG:
                nc.scalar.copy(
                    out=xw[s, r][:].rearrange("p g r k -> p (g r k)").bitcast(F32).rearrange("p (g r u) -> p g r u", g=G, u=2),
                    in_=b[:].rearrange("p (g u r) -> p g r u", g=G, u=2),
                )
            else:
                for g in range(G):
                    nc.vector.tensor_tensor(
                        out=xw[s, r][:, g].rearrange("p r (u e) -> p r u e", e=2),
                        in0=b[:, 256 * g : 256 * (g + 1)].bitcast(BF16).rearrange("p (u r e) -> p r u e", u=2, e=2),
                        in1=sc[:, g : g + 1, :].rearrange("p g (u e) -> p g u e", e=2).to_broadcast([P, P, 2, 2]),
                        op=MULT,
                    )

        def quant(s, r, src, codes, planes, bufs):
            codes[s, r] = work.tile([P, 256], U32, name="q", bufs=16, align_bytes=64)
            planes[s, r] = work.tile([P, 256], U8, name="s", bufs=16, align_bytes=64)
            nc.vector.quantize_mx(
                out=codes[s, r][:].bitcast(FP8X4), scales=planes[s, r][:], in_=src.rearrange("p g r k -> p (g r k)")
            )

        def quant_x(s, r):
            quant(s, r, xw[s, r][:], xq, xs, 8)

        def quant_h(s, r):
            quant(s, r, hb[s, r][:], hq, hs, 8)

        def hidden(s, r, c):
            b = bank["h", s, r, c] = psum.tile([P, 512], F32, name="bank")
            for t in range(4):
                for g in range(G):
                    cols = slice(P * g, P * (g + 1))
                    nc.tensor.matmul_mx(
                        out=b[:, P * t : P * (t + 1)],
                        lhsT=wop[:, c, g, t, :].bitcast(FP4X4),
                        lhsT_scale=wosp[:, c, g, t, :],
                        rhs=xq[s, r][:, cols].bitcast(FP8X4),
                        rhs_scale=xs[s, r][:, cols],
                        start=(g == 0),
                        stop=(g == G - 1),
                    )

        def add_bias(s, r, c):
            if (s, r) not in hb:
                hb[s, r] = work.tile([P, 2, P, 4], BF16, name="hb", align_bytes=64)
            dst = hb[s, r][:, c]
            src = bank["h", s, r, c][:].rearrange("p (t n) -> p n t", t=4)
            if (s, r, c) in HID_SCALAR:
                for t in range(4):
                    nc.scalar.activation(
                        dst[:, :, t], src[:, :, t], IDENTITY, bias=nbot[:, c, t : t + 1], scale=1.0 if s else -1.0
                    )
                return
            eng = nc.vector
            if (s, r, c) in HID_GPSIMD:
                raw = work.tile([P, P, 4], F32, name="raw")
                nc.scalar.copy(out=raw[:], in_=src)
                src = raw[:]
                eng = nc.gpsimd
            if s:
                eng.tensor_tensor(out=dst, in0=src, in1=bot[:, c : c + 1, :].to_broadcast([P, P, 4]), op=ADD)
            else:
                eng.tensor_tensor(out=dst, in0=nbot[:, c : c + 1, :].to_broadcast([P, P, 4]), in1=src, op=SUB)

        def project(key, r, e, streams):
            b = bank[key, r, e] = psum.tile([P, 512], F32, name="bank")
            passes = [(s, g) for s in streams for g in range(G)]
            for s, g in passes:
                cols = slice(P * g, P * (g + 1))
                nc.tensor.matmul_mx(
                    out=b[:],
                    lhsT=hq[s, r][:, cols].bitcast(FP8X4),
                    lhsT_scale=hs[s, r][:, cols],
                    rhs=wpw[:, g, 1024 * e : 1024 * (e + 1)].bitcast(FP4X4),
                    rhs_scale=wps[:, K * g + 512 * e : K * g + 512 * (e + 1)],
                    start=(s, g) == passes[0],
                    stop=(s, g) == passes[-1],
                )

        def pos_bank(r, e):
            project("p", r, e, (POS,))

        def diff_bank(r, e):
            project("d", r, e, (POS, NEG))

        def half(e):
            return slice(512 * e, 512 * (e + 1))

        def pos_out(r, e):
            if e == 0:
                pt[r] = work.tile([P, K], F32, name="pt")
                xxt[r] = work.tile([P, 2], F32, name="xx")
            if r in POS_VECTOR:
                nc.vector.tensor_tensor(out=pt[r][:, half(e)], in0=bank["p", r, e][:], in1=bpt[:, half(e)], op=ADD)
            else:
                raw = work.tile([P, P, 4], F32, name="raw")
                flat = raw[:].rearrange("p n t -> p (n t)")
                nc.scalar.copy(out=flat, in_=bank["p", r, e][:])
                nc.gpsimd.tensor_tensor(out=pt[r][:, half(e)], in0=flat, in1=bpt[:, half(e)], op=ADD)
            nc.sync.dma_start(out=out_0[r].rearrange("l p e -> (l p) e")[:, half(e)], in_=pt[r][:, half(e)])

        def square(r, e):
            sq = work.tile([P, 512], F32, name="sq", bufs=2)
            nc.scalar.activation(sq[:], pt[r][:, half(e)], SQUARE, accum_out=xxt[r][:, e : e + 1])

        def dot(r, e):
            if e == 0:
                st[r] = work.tile([P, 8], F32, name="st")
            jk = work.tile([P, 512], F32, name="junk", bufs=2)
            nc.vector.scalar_tensor_tensor(
                out=jk[:], in0=bank["d", r, e][:], scalar=1.0, in1=pt[r][:, half(e)], op0=MULT, op1=MULT,
                accum_out=st[r][:, e : e + 1],
            )

        def den(r):
            nc.vector.scalar_tensor_tensor(
                out=st[r][:, 2:3], in0=xxt[r][:, 0:1], scalar=EPS, in1=xxt[r][:, 1:2], op0=ADD, op1=ADD
            )

        def first_dot(r):
            nc.vector.tensor_scalar(out=st[r][:, 4:5], in0=st[r][:, 0:1], scalar1=EPS, scalar2=None, op0=ADD)

        def inverse(r):
            nc.vector.reciprocal(st[r][:, 3:4], st[r][:, 2:3])

        def coeff(r):
            s = st[r]
            nc.vector.tensor_scalar(
                out=s[:, 5:6], in0=s[:, 1:2], scalar1=s[:, 4:5], scalar2=s[:, 3:4], op0=ADD, op1=MULT
            )

        def neg_out(r, e):
            if e == 0:
                ot[r] = work.tile([P, K], F32, name="ot")
            nc.vector.scalar_tensor_tensor(
                out=ot[r][:, half(e)], in0=pt[r][:, half(e)], scalar=st[r][:, 5:6], in1=bank["d", r, e][:],
                op0=MULT, op1=SUB,
            )
            nc.sync.dma_start(out=out_1[r].rearrange("l p e -> (l p) e")[:, half(e)], in_=ot[r][:, half(e)])

        turn(NEG, 0)
        take(NEG, 0)
        for c in (1, 0):
            perm_words(c)
        for c in (1, 0):
            perm_scales(c)
        for r in range(R):
            widen(r)
        quant_x(NEG, 0)
        for r in range(R):
            if r + 1 < R:
                turn(NEG, r + 1)
                take(NEG, r + 1)
            turn(POS, r)
        for r in range(R):
            take(POS, r)
            if r + 1 < R:
                quant_x(NEG, r + 1)
            quant_x(POS, r)
        for i in range(R):
            for c in (1, 0):
                hidden(NEG, i, c)
                hidden(POS, i, c)
            add_bias(NEG, i, 1)
            add_bias(POS, i, 1)
            if i > 0:
                quant_h(POS, i - 1)
            add_bias(NEG, i, 0)
            if i > 0:
                quant_h(NEG, i - 1)
            add_bias(POS, i, 0)
            if i == R - 2:
                for e in range(2):
                    pos_bank(0, e)
                    pos_out(0, e)
                square(0, 0)
        for j in range(R + 1):
            for e in range(2):
                if j < R:
                    diff_bank(j, e)
                    dot(j, e)
                if (j, e) == (0, 0):
                    quant_h(POS, R - 1)
                    quant_h(NEG, R - 1)
                if j + 1 < R:
                    pos_bank(j + 1, e)
                    pos_out(j + 1, e)
                if j < R and e == 0:
                    square(j, 1)
                    den(j)
                if j + 1 < R and e == 1:
                    square(j + 1, 0)
                if j < R and e == 1:
                    first_dot(j)
                    inverse(j)
                if j > 0:
                    neg_out(j - 1, e)
            if j < R:
                coeff(j)
